import numpy as np
import ml_dtypes


def mxq(x, axis, fmt="e4m3"):
    dtype, down = {"e4m3": (ml_dtypes.float8_e4m3fn, 7), "e5m2": (ml_dtypes.float8_e5m2, 14)}[fmt]
    v = np.moveaxis(np.asarray(x, np.float32).astype(ml_dtypes.bfloat16).astype(np.float64), axis, -1)
    blocks = v.reshape(v.shape[:-1] + (-1, 32))
    amax = np.abs(blocks).max(-1, keepdims=True)
    byte = np.maximum(np.where(amax > 0, np.frexp(amax)[1] - 1 + 127, 0) - down, 1)
    scale = np.exp2(byte - 127.0)
    codes = (blocks / scale).astype(np.float32).astype(dtype).astype(np.float64)
    return np.moveaxis((codes * scale).reshape(v.shape), -1, axis)


WIDE = False


def mx_kscale(k):
    if not WIDE:
        return np.ones(k)
    levels = np.array([10, -10, 5, -5, 0])
    a = np.random.permutation(np.resize(levels, k // 512 * 4)).reshape(k // 512, 4)
    idx = np.arange(k)
    return np.exp2(a[idx // 512, idx % 128 // 32])


BF16 = ml_dtypes.bfloat16


def bf(x):
    return np.asarray(x, np.float32).astype(BF16)


def f64(x):
    return np.asarray(x).astype(np.float64)


E2M1 = np.array([0.0, 0.5, 1.0, 1.5, 2.0, 3.0, 4.0, 6.0, -0.0, -0.5, -1.0, -1.5, -2.0, -3.0, -4.0, -6.0])


def pack_weight(w, fmt):
    k, n = w.shape
    w = f64(bf(w)).reshape(k // 32, 32, n)
    amax = np.abs(w).max(1)
    if fmt == "e4m3":
        byte = np.frexp(amax)[1] - 1 + 127 - 7
    else:
        mant, ex = np.frexp(amax / 6.0)
        byte = np.where(mant > 0.5, ex, ex - 1) + 127
    byte = np.clip(np.where(amax > 0, byte, 1), 1, 254)
    scaled = (w * np.exp2(127.0 - byte)[:, None, :]).reshape(k, n).astype(np.float32)
    by_word = np.ascontiguousarray(scaled.reshape(k // 512, 128, 4, n).transpose(0, 1, 3, 2))
    if fmt == "e4m3":
        words = by_word.astype(ml_dtypes.float8_e4m3fn).view(np.uint8)
    else:
        c = by_word.astype(ml_dtypes.float4_e2m1fn).view(np.uint8) & 0xF
        words = c[..., 0::2] | (c[..., 1::2] << 4)
    return np.ascontiguousarray(words), np.ascontiguousarray(byte.astype(np.uint8).reshape(k // 512, 16, n))


def unpack_weight(words, scales, fmt):
    g, p, n, _ = words.shape
    if fmt == "e4m3":
        vals = np.ascontiguousarray(words).view(ml_dtypes.float8_e4m3fn).astype(np.float64)
    else:
        nib = np.empty((g, p, n, 4), np.uint8)
        nib[..., 0::2] = words & 0xF
        nib[..., 1::2] = words >> 4
        vals = E2M1[nib]
    vals = vals * np.repeat(np.exp2(scales.astype(np.float64) - 127.0), 8, axis=1)[..., None]
    return vals.transpose(0, 1, 3, 2).reshape(g * 512, n)

def pack4(w):
    words, scales = pack_weight(w, "e2m1")
    return words.reshape(words.shape[0], 128, -1), scales


def unpack4(words, scales):
    return unpack_weight(words.reshape(words.shape[0], 128, -1, 2), scales, "e2m1")


B, F, L, SEG, PRED, D, H = 64, 128, 48, 24, 192, 512, 1024
R = B * F
EPS = 1e-15
MAXN = 1.0 - 1e-5


def norm(a):
    return np.sqrt(np.maximum(np.sum(a * a, axis=-1, keepdims=True), EPS))


def artanh(r):
    c = np.clip(r, -1.0 + 1e-7, 1.0 - 1e-7)
    return 0.5 * np.log((1.0 + c) / (1.0 - c))


def projx(a):
    n = norm(a)
    return np.where(n > MAXN, a * (MAXN / n), a)


def expmap0(v):
    n = norm(v)
    return np.tanh(n) * v / n


def mobius_add(x, y):
    x2 = np.sum(x * x, -1, keepdims=True)
    y2 = np.sum(y * y, -1, keepdims=True)
    xy = np.sum(x * y, -1, keepdims=True)
    num = (1.0 + 2.0 * xy + y2) * x + (1.0 - x2) * y
    den = 1.0 + 2.0 * xy + x2 * y2
    return num / np.maximum(den, EPS)


def setup_inputs():
    s = mx_kscale(D)
    c = np.exp2(np.ceil(np.log2(np.sqrt(np.mean(s * s)))))
    v_init = bf(np.random.standard_normal((R, D)) * 0.55 / np.sqrt(D) * s / c)
    w = np.random.standard_normal((D, D)) * 1.5 / np.sqrt(D) * c / s[None, :]
    words, scales = pack4(np.ascontiguousarray(w.T))
    b_vel = bf(np.random.standard_normal(D) * 0.4 / np.sqrt(D))
    return {"v_init": v_init,
            "W_vel_words": words,
            "W_vel_scales": scales,
            "b_vel": b_vel}


def reference(v_init, W_vel_words, W_vel_scales, b_vel):
    x = f64(v_init)
    mx = mxq(x, 1, "e4m3") @ unpack4(W_vel_words, W_vel_scales)
    xn = norm(x)
    mxn = norm(mx)
    p = np.tanh(mxn / xn * artanh(xn)) * mx / mxn
    return projx(mobius_add(p, expmap0(f64(b_vel))))

@@ -1,0 +1,367 @@
+from contextlib import ExitStack
+
+import concourse.mybir as mybir
+from concourse.masks import make_identity
+
+F32 = mybir.dt.float32
+BF16 = mybir.dt.bfloat16
+I32 = mybir.dt.int32
+U32 = mybir.dt.uint32
+U8 = mybir.dt.uint8
+FP8X4 = mybir.dt.float8_e4m3fn_x4
+FP4X4 = mybir.dt.float4_e2m1fn_x4
+ALU = mybir.AluOpType
+ACT = mybir.ActivationFunctionType
+
+P = 128
+PACK = 4
+ROWS = 8192
+D = 512
+TILES = ROWS // P
+GROUP = 4
+GROUPS = TILES // GROUP
+BATCH = 16
+BATCHES = TILES // BATCH
+WORDS = D // 2
+
+POW_ROUNDS = 7
+ROUNDS = 18 + POW_ROUNDS
+Q_ROWS_AHEAD = 3
+LAG = BATCH - 1 + ROUNDS // 2 + Q_ROWS_AHEAD
+FEED_AHEAD = 2
+X_AHEAD = 8
+
+EPS = 1e-15
+MAXN = 1.0 - 1e-5
+CLIP = 1.0 - 1e-7
+TWO_LOG2E = 2.8853900817779268
+
+FLOPS = 2 * ROWS * D * D
+
+
+def tile_directnodecomphyperbolicforecaster_pa_t_kernel(
+    tc, v_init, W_vel_words, W_vel_scales, b_vel, out
+):
+    nc = tc.nc
+    x_rows = v_init.rearrange("(p t) k -> p t k", t=TILES)
+    out_rows = out.rearrange("(p t) n -> p t n", t=TILES)
+
+    with ExitStack() as ctx:
+        keep = ctx.enter_context(tc.tile_pool(name="keep", bufs=1))
+        stage = ctx.enter_context(tc.tile_pool(name="stage", bufs=3))
+        unread = ctx.enter_context(tc.tile_pool(name="unread", bufs=3))
+        chain = ctx.enter_context(tc.tile_pool(name="chain", bufs=2))
+        bias_rows = ctx.enter_context(tc.tile_pool(name="bias_rows", bufs=Q_ROWS_AHEAD + 2))
+        results = ctx.enter_context(tc.tile_pool(name="results", bufs=3))
+        psum_t = ctx.enter_context(tc.psum_pool(name="psum_t", bufs=2))
+        psum_a = ctx.enter_context(tc.psum_pool(name="psum_a", bufs=3))
+        psum_b = ctx.enter_context(tc.psum_pool(name="psum_b", bufs=3))
+        ctx.enter_context(tc.manual_schedule())
+
+        x_sb = keep.tile([P, TILES, D], BF16, name="x_sb")
+        x_words = x_sb[:].bitcast(F32)
+        x_codes = keep.tile([P, TILES * P], U32, name="x_codes", align_bytes=64)
+        x_scales = keep.tile([P, TILES * P], U8, name="x_scales", align_bytes=64)
+        w_words = keep.tile([P, 2 * D], U8, name="w_words", align_bytes=64)
+        w_scales = keep.tile([P, D], U8, name="w_scales", align_bytes=64)
+        ident = keep.tile([P, P], F32, name="ident")
+        b_all = keep.tile([P, D], BF16, name="b_all")
+        q_all = keep.tile([P, D], F32, name="q_all")
+        two = keep.tile([P, 1], F32, name="two")
+        warm = keep.tile([P, 1], F32, name="warm")
+        sums = keep.tile([P, 2, TILES], F32, name="sums")
+        mx_dot_q = keep.tile([P, TILES], F32, name="mx_dot_q")
+        coef_mx = keep.tile([P, TILES], F32, name="coef_mx")
+        coef_q = keep.tile([P, TILES], F32, name="coef_q")
+        q_sq = keep.tile([P, 1], F32, name="q_sq")
+        q_sq_m1 = keep.tile([P, 1], F32, name="q_sq_m1")
+
+        nc.vector.memset(w_scales[:].bitcast(I32), 0)
+        nc.vector.memset(two[:], 2.0)
+        nc.vector.memset(warm[:], 1.0)
+        nc.scalar.activation(out=warm[:], in_=warm[:], func=ACT.Sqrt)
+        make_identity(nc, ident[:])
+
+        def load_group(g):
+            tiles = slice(g * GROUP, (g + 1) * GROUP)
+            nc.sync.dma_start(out=x_sb[:, tiles, :], in_=x_rows[:, tiles, :])
+
+        load_group(0)
+        nc.scalar.dma_start(out=b_all[:], in_=b_vel.partition_broadcast(P))
+        nc.sync.dma_start(out=w_words[:].bitcast(I32), in_=W_vel_words[0].bitcast(I32))
+        for quad in range(4):
+            nc.sync.dma_start(
+                out=w_scales[32 * quad : 32 * quad + 4, :].bitcast(I32),
+                in_=W_vel_scales[0, 4 * quad : 4 * quad + 4, :].bitcast(I32),
+            )
+        for g in range(1, GROUPS):
+            load_group(g)
+
+        def small(name, width=BATCH):
+            return chain.tile([P, width], F32, name=name)
+
+        transposed = {}
+        regrouped = {}
+
+        def transpose_group(g):
+            transposed[g] = []
+            for half in range(GROUP // 2):
+                xt = psum_t.tile([P, 2, 2, P], F32, name="xt")
+                for j in range(2):
+                    t = g * GROUP + 2 * half + j
+                    for u in range(2):
+                        nc.tensor.transpose(xt[:, j, u, :], x_words[:, t, u:WORDS:2], ident[:])
+                transposed[g].append(xt)
+
+        def regroup_half(g, half, on_vector):
+            if half == 0:
+                regrouped[g] = stage.tile([P, GROUP, P, PACK], BF16, name="grouped", align_bytes=64)
+            grouped_words = regrouped[g][:].bitcast(F32)
+            dst = grouped_words[:, 2 * half : 2 * half + 2, :, :]
+            src = transposed[g][half][:].rearrange("p j u r -> p j r u")
+            if on_vector:
+                nc.vector.tensor_copy(out=dst, in_=src)
+            else:
+                nc.scalar.copy(out=dst, in_=src)
+
+        def quantise_group(g):
+            cols = slice(g * GROUP * P, (g + 1) * GROUP * P)
+            nc.vector.quantize_mx(
+                out=x_codes[:, cols].bitcast(FP8X4),
+                scales=x_scales[:, cols],
+                in_=regrouped[g][:].rearrange("p j r t -> p (j r t)"),
+            )
+
+        def product(acc, t):
+            rows = slice(t * P, (t + 1) * P)
+            nc.tensor.matmul_mx(
+                out=acc,
+                lhsT=x_codes[:, rows].bitcast(FP8X4),
+                lhsT_scale=x_scales[:, rows],
+                rhs=w_words[:].bitcast(FP4X4),
+                rhs_scale=w_scales[:],
+                start=True,
+                stop=True,
+            )
+
+        def sum_squares(values, total):
+            squares = unread.tile([P, D], F32, name="by_scalar")
+            nc.scalar.activation(out=squares[:], in_=values, func=ACT.Square, accum_out=total)
+
+        def sum_mx_times_q(acc, t):
+            products = unread.tile([P, D], F32, name="by_vector")
+            nc.vector.scalar_tensor_tensor(
+                out=products[:], in0=acc, scalar=1.0, in1=q_all[:], op0=ALU.mult, op1=ALU.mult,
+                accum_out=mx_dot_q[:, t : t + 1],
+            )
+
+        def coefficient_rounds(b):
+            cols = slice(b * BATCH, (b + 1) * BATCH)
+            vec = nc.vector
+            sq = chain.tile([P, 2, BATCH], F32, name="sq")
+            norms = chain.tile([P, 2, BATCH], F32, name="norms")
+            inv_norms = chain.tile([P, 2, BATCH], F32, name="inv_norms")
+            xn, mxn = norms[:, 0, :], norms[:, 1, :]
+            inv_xn, inv_mxn = inv_norms[:, 0, :], inv_norms[:, 1, :]
+            one_plus_c, c_minus_one = small("one_plus_c"), small("c_minus_one")
+            inv_c_minus_one, rho, kappa = small("inv_c_minus_one"), small("rho"), small("kappa")
+            power, power_plus_one, inverse = small("power"), small("power_plus_one"), small("inverse")
+            neg_tanh, neg_a, pp, neg_pq = small("neg_tanh"), small("neg_a"), small("pp"), small("neg_pq")
+            one_2pq, den_raw, den, inv_den = small("one_2pq"), small("den_raw"), small("den"), small("inv_den")
+            s_pq, neg_c_p_a, mm, mm_clamped = small("s_pq"), small("neg_c_p_a"), small("mm"), small("mm_clamped")
+            m_norm, inv_m_norm = small("m_norm"), small("inv_m_norm")
+            shrink, neg_common = small("shrink"), small("neg_common")
+            mult, add = ALU.mult, ALU.add
+
+            norms_and_rho = [
+                [
+                    lambda: vec.tensor_scalar_max(out=sq[:], in0=sums[:, :, cols], scalar1=EPS),
+                    lambda: nc.scalar.activation(out=norms[:], in_=sq[:], func=ACT.Sqrt),
+                ],
+                [
+                    lambda: vec.reciprocal(out=inv_norms[:], in_=norms[:]),
+                    lambda: vec.tensor_scalar(
+                        out=one_plus_c[:], in0=xn, scalar1=CLIP, scalar2=1.0, op0=ALU.min, op1=add
+                    ),
+                    lambda: vec.tensor_scalar(
+                        out=c_minus_one[:], in0=xn, scalar1=CLIP, scalar2=1.0,
+                        op0=ALU.min, op1=ALU.subtract,
+                    ),
+                ],
+                [
+                    lambda: vec.reciprocal(out=inv_c_minus_one[:], in_=c_minus_one[:]),
+                    lambda: vec.tensor_mul(out=kappa[:], in0=mxn, in1=inv_xn),
+                ],
+                [
+                    lambda: vec.scalar_tensor_tensor(
+                        out=rho[:], in0=one_plus_c[:], scalar=-1.0, in1=inv_c_minus_one[:],
+                        op0=mult, op1=mult,
+                    ),
+                    lambda: nc.gpsimd.tensor_tensor(
+                        out=power[:], in0=rho[:], in1=kappa[:], op=ALU.pow
+                    ),
+                    lambda: nc.gpsimd.tensor_scalar(
+                        out=power_plus_one[:], in0=power[:], scalar1=1.0, scalar2=1.0,
+                        op0=add, op1=mult,
+                    ),
+                ],
+            ]
+            while_gpsimd_works = [[] for i in range(POW_ROUNDS)]
+            moebius = [
+                [lambda: vec.reciprocal(out=inverse[:], in_=power_plus_one[:])],
+                [
+                    lambda: vec.tensor_scalar(
+                        out=neg_tanh[:], in0=inverse[:], scalar1=2.0, scalar2=-1.0, op0=mult, op1=add
+                    )
+                ],
+                [
+                    lambda: vec.tensor_mul(out=neg_a[:], in0=neg_tanh[:], in1=inv_mxn),
+                    lambda: vec.tensor_mul(out=pp[:], in0=neg_tanh[:], in1=neg_tanh[:]),
+                ],
+                [lambda: vec.tensor_mul(out=neg_pq[:], in0=neg_a[:], in1=mx_dot_q[:, cols])],
+                [
+                    lambda: vec.tensor_scalar(
+                        out=one_2pq[:], in0=neg_pq[:], scalar1=-2.0, scalar2=1.0, op0=mult, op1=add
+                    )
+                ],
+                [
+                    lambda: vec.scalar_tensor_tensor(
+                        out=den_raw[:], in0=pp[:], scalar=q_sq[:, 0:1], in1=one_2pq[:],
+                        op0=mult, op1=add,
+                    ),
+                    lambda: vec.scalar_tensor_tensor(
+                        out=s_pq[:], in0=pp[:], scalar=q_sq_m1[:, 0:1], in1=one_2pq[:],
+                        op0=add, op1=add,
+                    ),
+                    lambda: vec.scalar_tensor_tensor(
+                        out=neg_c_p_a[:], in0=one_2pq[:], scalar=q_sq[:, 0:1], in1=neg_a[:],
+                        op0=add, op1=mult,
+                    ),
+                ],
+                [lambda: vec.tensor_scalar_max(out=den[:], in0=den_raw[:], scalar1=EPS)],
+                [lambda: vec.reciprocal(out=inv_den[:], in_=den[:])],
+                [lambda: vec.tensor_mul(out=mm[:], in0=s_pq[:], in1=inv_den[:])],
+                [
+                    lambda: vec.tensor_scalar_max(out=mm_clamped[:], in0=mm[:], scalar1=EPS),
+                    lambda: nc.scalar.activation(out=m_norm[:], in_=mm_clamped[:], func=ACT.Sqrt),
+                ],
+            ]
+            projection = [
+                [lambda: vec.reciprocal(out=inv_m_norm[:], in_=m_norm[:])],
+                [
+                    lambda: vec.tensor_scalar(
+                        out=shrink[:], in0=inv_m_norm[:], scalar1=MAXN, scalar2=1.0,
+                        op0=mult, op1=ALU.min,
+                    )
+                ],
+                [
+                    lambda: vec.scalar_tensor_tensor(
+                        out=neg_common[:], in0=shrink[:], scalar=-1.0, in1=inv_den[:],
+                        op0=mult, op1=mult,
+                    )
+                ],
+                [
+                    lambda: vec.scalar_tensor_tensor(
+                        out=coef_q[:, cols], in0=pp[:], scalar=1.0, in1=neg_common[:],
+                        op0=ALU.subtract, op1=mult,
+                    ),
+                    lambda: vec.tensor_mul(out=coef_mx[:, cols], in0=neg_c_p_a[:], in1=neg_common[:]),
+                ],
+            ]
+            return norms_and_rho + while_gpsimd_works + moebius + projection
+
+        rounds = {}
+
+        def issue_round(b, k):
+            if b in rounds and 0 <= k < ROUNDS:
+                for issue in rounds[b][k]:
+                    issue()
+
+        q_rows = {}
+        result = {}
+
+        def scale_q(t, on_scalar):
+            q_rows[t] = bias_rows.tile([P, D], F32, name="q_row")
+            if on_scalar:
+                nc.scalar.activation(
+                    out=q_rows[t][:], in_=q_all[:], func=ACT.Copy, scale=coef_q[:, t : t + 1]
+                )
+            else:
+                nc.gpsimd.tensor_scalar(
+                    out=q_rows[t][:], in0=q_all[:], scalar1=coef_q[:, t : t + 1], scalar2=0.0,
+                    op0=ALU.mult, op1=ALU.add,
+                )
+
+        def write_tile(t):
+            g, j = divmod(t, GROUP)
+            if j == 0:
+                result[g] = results.tile([P, GROUP, D], F32, name="result")
+            acc_b = psum_b.tile([P, D], F32, name="acc_b")
+            product(acc_b[:], t)
+            nc.vector.scalar_tensor_tensor(
+                out=result[g][:, j, :], in0=acc_b[:], scalar=coef_mx[:, t : t + 1], in1=q_rows[t][:],
+                op0=ALU.mult, op1=ALU.add,
+            )
+            if j == GROUP - 1:
+                tiles = slice(g * GROUP, (g + 1) * GROUP)
+                nc.sync.dma_start(out=out_rows[:, tiles, :], in_=result[g][:])
+
+        b_sq, b_sq_clamped, b_norm = small("b_sq", 1), small("b_sq_clamped", 1), small("b_norm", 1)
+        b_exponent, b_power = small("b_exponent", 1), small("b_power", 1)
+        b_above, b_below, b_inv_below = small("b_above", 1), small("b_below", 1), small("b_inv_below", 1)
+        q_scale = small("q_scale", 1)
+        sum_squares(b_all[:], b_sq[:])
+        nc.vector.tensor_scalar_max(out=b_sq_clamped[:], in0=b_sq[:], scalar1=EPS)
+        nc.scalar.activation(out=b_norm[:], in_=b_sq_clamped[:], func=ACT.Sqrt)
+        nc.vector.tensor_scalar_mul(out=b_exponent[:], in0=b_norm[:], scalar1=TWO_LOG2E)
+        nc.gpsimd.tensor_tensor(out=b_power[:], in0=two[:], in1=b_exponent[:], op=ALU.pow)
+        transpose_group(0)
+        regroup_half(0, 0, True)
+        regroup_half(0, 1, True)
+        quantise_group(0)
+        nc.vector.tensor_scalar_add(out=b_above[:], in0=b_power[:], scalar1=-1.0)
+        nc.vector.scalar_tensor_tensor(
+            out=b_below[:], in0=b_power[:], scalar=1.0, in1=b_norm[:], op0=ALU.add, op1=ALU.mult
+        )
+        nc.vector.reciprocal(out=b_inv_below[:], in_=b_below[:])
+        nc.vector.tensor_mul(out=q_scale[:], in0=b_above[:], in1=b_inv_below[:])
+        nc.vector.tensor_scalar_mul(out=q_all[:], in0=b_all[:], scalar1=q_scale[:, 0:1])
+        for g in range(1, FEED_AHEAD):
+            transpose_group(g)
+            regroup_half(g, 0, True)
+            regroup_half(g, 1, True)
+            quantise_group(g)
+        for t in range(X_AHEAD):
+            sum_squares(x_sb[:, t, :], sums[:, 0, t : t + 1])
+        sum_squares(q_all[:], q_sq[:])
+        nc.vector.tensor_scalar_add(out=q_sq_m1[:], in0=q_sq[:], scalar1=-1.0)
+
+        for s in range(TILES + LAG):
+            batches_done, since = divmod(s + 1, BATCH)
+            b = batches_done - 1
+            if s < TILES:
+                acc = psum_a.tile([P, D], F32, name="acc_a")
+                product(acc[:], s)
+                sum_squares(acc[:], sums[:, 1, s : s + 1])
+            if s >= LAG:
+                write_tile(s - LAG)
+            issue_round(b, 2 * since - 1)
+            if s < TILES:
+                sum_mx_times_q(acc[:], s)
+                g, j = divmod(s, GROUP)
+                if g + FEED_AHEAD < GROUPS:
+                    if j == 0:
+                        transpose_group(g + FEED_AHEAD)
+                    elif j == GROUP - 1:
+                        quantise_group(g + FEED_AHEAD)
+                    else:
+                        regroup_half(g + FEED_AHEAD, j - 1, s < LAG)
+                if s + X_AHEAD < TILES:
+                    sum_squares(x_sb[:, s + X_AHEAD, :], sums[:, 0, s + X_AHEAD : s + X_AHEAD + 1])
+            if since == 0 and b < BATCHES:
+                rounds[b] = coefficient_rounds(b)
+                assert len(rounds[b]) == ROUNDS
+            issue_round(b, 2 * since)
+            t = s - LAG + Q_ROWS_AHEAD
+            if 0 <= t < TILES:
+                scale_q(t, s >= TILES and t % 2 == 1)

@@ -24,12 +24,13 @@ BATCH = 16
 BATCHES = TILES // BATCH
 WORDS = D // 2
 
-POW_ROUNDS = 7
-ROUNDS = 18 + POW_ROUNDS
+POW_ROUNDS = 9
+ROUNDS = 15 + POW_ROUNDS
 Q_ROWS_AHEAD = 3
 LAG = BATCH - 1 + ROUNDS // 2 + Q_ROWS_AHEAD
 FEED_AHEAD = 2
 X_AHEAD = 8
+HOLD = 4
 
 EPS = 1e-15
 MAXN = 1.0 - 1e-5
@@ -86,7 +87,8 @@ def tile_directnodecomphyperbolicforecaster_pa_t_kernel(
             tiles = slice(g * GROUP, (g + 1) * GROUP)
             nc.sync.dma_start(out=x_sb[:, tiles, :], in_=x_rows[:, tiles, :])
 
-        load_group(0)
+        for t in range(GROUP):
+            nc.sync.dma_start(out=x_sb[:, t, :], in_=x_rows[:, t, :])
         nc.scalar.dma_start(out=b_all[:], in_=b_vel.partition_broadcast(P))
         nc.sync.dma_start(out=w_words[:].bitcast(I32), in_=W_vel_words[0].bitcast(I32))
         for quad in range(4):
@@ -155,22 +157,28 @@ def tile_directnodecomphyperbolicforecaster_pa_t_kernel(
                 accum_out=mx_dot_q[:, t : t + 1],
             )
 
-        def coefficient_rounds(b):
+        def coefficient_rounds(b, pow_rounds):
             cols = slice(b * BATCH, (b + 1) * BATCH)
             vec = nc.vector
             sq = chain.tile([P, 2, BATCH], F32, name="sq")
             norms = chain.tile([P, 2, BATCH], F32, name="norms")
-            inv_norms = chain.tile([P, 2, BATCH], F32, name="inv_norms")
             xn, mxn = norms[:, 0, :], norms[:, 1, :]
-            inv_xn, inv_mxn = inv_norms[:, 0, :], inv_norms[:, 1, :]
-            one_plus_c, c_minus_one = small("one_plus_c"), small("c_minus_one")
-            inv_c_minus_one, rho, kappa = small("inv_c_minus_one"), small("rho"), small("kappa")
+            factors = chain.tile([P, 4, BATCH], F32, name="factors")
+            inv_xn, inv_mxn, dot_over_mxn, neg_tanh = (
+                factors[:, 0, :], factors[:, 1, :], factors[:, 2, :], factors[:, 3, :]
+            )
+            products = chain.tile([P, 3, BATCH], F32, name="products")
+            neg_a, neg_pq, pp = products[:, 0, :], products[:, 1, :], products[:, 2, :]
+            c_minus_one, inv_c_minus_one = small("c_minus_one"), small("inv_c_minus_one")
+            rho, kappa = small("rho"), small("kappa")
             power, power_plus_one, inverse = small("power"), small("power_plus_one"), small("inverse")
-            neg_tanh, neg_a, pp, neg_pq = small("neg_tanh"), small("neg_a"), small("pp"), small("neg_pq")
-            one_2pq, den_raw, den, inv_den = small("one_2pq"), small("den_raw"), small("den"), small("inv_den")
-            s_pq, neg_c_p_a, mm, mm_clamped = small("s_pq"), small("neg_c_p_a"), small("mm"), small("mm_clamped")
-            m_norm, inv_m_norm = small("m_norm"), small("inv_m_norm")
-            shrink, neg_common = small("shrink"), small("neg_common")
+            one_2pq, neg_c_p_a = small("one_2pq"), small("neg_c_p_a")
+            pair = chain.tile([P, 2, BATCH], F32, name="pair")
+            neg_pair = chain.tile([P, 2, BATCH], F32, name="neg_pair")
+            neg_inv_pair = chain.tile([P, 2, BATCH], F32, name="neg_inv_pair")
+            neg_inv_den = neg_inv_pair[:, 0, :]
+            inv_mm, inv_m_norm = small("inv_mm"), small("inv_m_norm")
+            neg_scaled, neg_common = small("neg_scaled"), small("neg_common")
             mult, add = ALU.mult, ALU.add
 
             norms_and_rho = [
@@ -179,10 +187,7 @@ def tile_directnodecomphyperbolicforecaster_pa_t_kernel(
                     lambda: nc.scalar.activation(out=norms[:], in_=sq[:], func=ACT.Sqrt),
                 ],
                 [
-                    lambda: vec.reciprocal(out=inv_norms[:], in_=norms[:]),
-                    lambda: vec.tensor_scalar(
-                        out=one_plus_c[:], in0=xn, scalar1=CLIP, scalar2=1.0, op0=ALU.min, op1=add
-                    ),
+                    lambda: vec.reciprocal(out=factors[:, 0:2, :], in_=norms[:]),
                     lambda: vec.tensor_scalar(
                         out=c_minus_one[:], in0=xn, scalar1=CLIP, scalar2=1.0,
                         op0=ALU.min, op1=ALU.subtract,
@@ -191,11 +196,11 @@ def tile_directnodecomphyperbolicforecaster_pa_t_kernel(
                 [
                     lambda: vec.reciprocal(out=inv_c_minus_one[:], in_=c_minus_one[:]),
                     lambda: vec.tensor_mul(out=kappa[:], in0=mxn, in1=inv_xn),
+                    lambda: vec.tensor_mul(out=dot_over_mxn, in0=mx_dot_q[:, cols], in1=inv_mxn),
                 ],
                 [
-                    lambda: vec.scalar_tensor_tensor(
-                        out=rho[:], in0=one_plus_c[:], scalar=-1.0, in1=inv_c_minus_one[:],
-                        op0=mult, op1=mult,
+                    lambda: vec.tensor_scalar(
+                        out=rho[:], in0=inv_c_minus_one[:], scalar1=-2.0, scalar2=-1.0, op0=mult, op1=add
                     ),
                     lambda: nc.gpsimd.tensor_tensor(
                         out=power[:], in0=rho[:], in1=kappa[:], op=ALU.pow
@@ -206,63 +211,61 @@ def tile_directnodecomphyperbolicforecaster_pa_t_kernel(
                     ),
                 ],
             ]
-            while_gpsimd_works = [[] for i in range(POW_ROUNDS)]
+            while_gpsimd_works = [[] for i in range(pow_rounds)]
             moebius = [
                 [lambda: vec.reciprocal(out=inverse[:], in_=power_plus_one[:])],
                 [
                     lambda: vec.tensor_scalar(
-                        out=neg_tanh[:], in0=inverse[:], scalar1=2.0, scalar2=-1.0, op0=mult, op1=add
+                        out=neg_tanh, in0=inverse[:], scalar1=2.0, scalar2=-1.0, op0=mult, op1=add
                     )
                 ],
                 [
-                    lambda: vec.tensor_mul(out=neg_a[:], in0=neg_tanh[:], in1=inv_mxn),
-                    lambda: vec.tensor_mul(out=pp[:], in0=neg_tanh[:], in1=neg_tanh[:]),
+                    lambda: vec.tensor_mul(
+                        out=products[:], in0=factors[:, 1:4, :],
+                        in1=factors[:, 3:4, :].to_broadcast([P, 3, BATCH]),
+                    )
                 ],
-                [lambda: vec.tensor_mul(out=neg_pq[:], in0=neg_a[:], in1=mx_dot_q[:, cols])],
                 [
                     lambda: vec.tensor_scalar(
-                        out=one_2pq[:], in0=neg_pq[:], scalar1=-2.0, scalar2=1.0, op0=mult, op1=add
+                        out=one_2pq[:], in0=neg_pq, scalar1=-2.0, scalar2=1.0, op0=mult, op1=add
                     )
                 ],
                 [
                     lambda: vec.scalar_tensor_tensor(
-                        out=den_raw[:], in0=pp[:], scalar=q_sq[:, 0:1], in1=one_2pq[:],
+                        out=pair[:, 0, :], in0=pp, scalar=q_sq[:, 0:1], in1=one_2pq[:],
                         op0=mult, op1=add,
                     ),
                     lambda: vec.scalar_tensor_tensor(
-                        out=s_pq[:], in0=pp[:], scalar=q_sq_m1[:, 0:1], in1=one_2pq[:],
+                        out=pair[:, 1, :], in0=pp, scalar=q_sq_m1[:, 0:1], in1=one_2pq[:],
                         op0=add, op1=add,
                     ),
                     lambda: vec.scalar_tensor_tensor(
-                        out=neg_c_p_a[:], in0=one_2pq[:], scalar=q_sq[:, 0:1], in1=neg_a[:],
+                        out=neg_c_p_a[:], in0=one_2pq[:], scalar=q_sq[:, 0:1], in1=neg_a,
                         op0=add, op1=mult,
                     ),
                 ],
-                [lambda: vec.tensor_scalar_max(out=den[:], in0=den_raw[:], scalar1=EPS)],
-                [lambda: vec.reciprocal(out=inv_den[:], in_=den[:])],
-                [lambda: vec.tensor_mul(out=mm[:], in0=s_pq[:], in1=inv_den[:])],
                 [
-                    lambda: vec.tensor_scalar_max(out=mm_clamped[:], in0=mm[:], scalar1=EPS),
-                    lambda: nc.scalar.activation(out=m_norm[:], in_=mm_clamped[:], func=ACT.Sqrt),
+                    lambda: vec.tensor_scalar(
+                        out=neg_pair[:], in0=pair[:], scalar1=EPS, scalar2=-1.0, op0=ALU.max, op1=mult
+                    )
+                ],
+                [lambda: vec.reciprocal(out=neg_inv_pair[:], in_=neg_pair[:])],
+                [
+                    lambda: vec.tensor_mul(out=inv_mm[:], in0=neg_pair[:, 0, :], in1=neg_inv_pair[:, 1, :]),
+                    lambda: nc.scalar.activation(out=inv_m_norm[:], in_=inv_mm[:], func=ACT.Sqrt),
                 ],
             ]
             projection = [
-                [lambda: vec.reciprocal(out=inv_m_norm[:], in_=m_norm[:])],
-                [
-                    lambda: vec.tensor_scalar(
-                        out=shrink[:], in0=inv_m_norm[:], scalar1=MAXN, scalar2=1.0,
-                        op0=mult, op1=ALU.min,
-                    )
-                ],
                 [
                     lambda: vec.scalar_tensor_tensor(
-                        out=neg_common[:], in0=shrink[:], scalar=-1.0, in1=inv_den[:],
+                        out=neg_scaled[:], in0=inv_m_norm[:], scalar=MAXN, in1=neg_inv_den,
                         op0=mult, op1=mult,
                     )
                 ],
+                [lambda: vec.tensor_max(out=neg_common[:], in0=neg_scaled[:], in1=neg_inv_den)],
                 [
                     lambda: vec.scalar_tensor_tensor(
-                        out=coef_q[:, cols], in0=pp[:], scalar=1.0, in1=neg_common[:],
+                        out=coef_q[:, cols], in0=pp, scalar=1.0, in1=neg_common[:],
                         op0=ALU.subtract, op1=mult,
                     ),
                     lambda: vec.tensor_mul(out=coef_mx[:, cols], in0=neg_c_p_a[:], in1=neg_common[:]),
@@ -273,7 +276,7 @@ def tile_directnodecomphyperbolicforecaster_pa_t_kernel(
         rounds = {}
 
         def issue_round(b, k):
-            if b in rounds and 0 <= k < ROUNDS:
+            if b in rounds and 0 <= k < len(rounds[b]):
                 for issue in rounds[b][k]:
                     issue()
 
@@ -332,19 +335,33 @@ def tile_directnodecomphyperbolicforecaster_pa_t_kernel(
             regroup_half(g, 1, True)
             quantise_group(g)
         for t in range(X_AHEAD):
-            sum_squares(x_sb[:, t, :], sums[:, 0, t : t + 1])
+            if t < X_AHEAD - 2:
+                sum_squares(x_sb[:, t, :], sums[:, 0, t : t + 1])
+            else:
+                squares = unread.tile([P, D], F32, name="by_vector")
+                nc.vector.scalar_tensor_tensor(
+                    out=squares[:], in0=x_sb[:, t, :], scalar=1.0, in1=x_sb[:, t, :],
+                    op0=ALU.mult, op1=ALU.mult, accum_out=sums[:, 0, t : t + 1],
+                )
         sum_squares(q_all[:], q_sq[:])
         nc.vector.tensor_scalar_add(out=q_sq_m1[:], in0=q_sq[:], scalar1=-1.0)
 
-        for s in range(TILES + LAG):
-            batches_done, since = divmod(s + 1, BATCH)
-            b = batches_done - 1
+        def written(s):
+            if s < TILES - HOLD:
+                return s - LAG if s >= LAG else None
+            if s < TILES:
+                return None
+            return s - LAG - HOLD if s - LAG - HOLD < TILES else None
+
+        for s in range(TILES + LAG + HOLD):
+            b = min((s + 1) // BATCH, BATCHES) - 1
+            since = s + 1 - (b + 1) * BATCH
             if s < TILES:
                 acc = psum_a.tile([P, D], F32, name="acc_a")
                 product(acc[:], s)
                 sum_squares(acc[:], sums[:, 1, s : s + 1])
-            if s >= LAG:
-                write_tile(s - LAG)
+            if written(s) is not None:
+                write_tile(written(s))
             issue_round(b, 2 * since - 1)
             if s < TILES:
                 sum_mx_times_q(acc[:], s)
@@ -358,10 +375,9 @@ def tile_directnodecomphyperbolicforecaster_pa_t_kernel(
                         regroup_half(g + FEED_AHEAD, j - 1, s < LAG)
                 if s + X_AHEAD < TILES:
                     sum_squares(x_sb[:, s + X_AHEAD, :], sums[:, 0, s + X_AHEAD : s + X_AHEAD + 1])
-            if since == 0 and b < BATCHES:
-                rounds[b] = coefficient_rounds(b)
-                assert len(rounds[b]) == ROUNDS
+            if since == 0:
+                rounds[b] = coefficient_rounds(b, POW_ROUNDS + (2 * HOLD if b == BATCHES - 1 else 0))
             issue_round(b, 2 * since)
-            t = s - LAG + Q_ROWS_AHEAD
-            if 0 <= t < TILES:
-                scale_q(t, s >= TILES and t % 2 == 1)
+            t = written(s + Q_ROWS_AHEAD)
+            if t is not None:
+                scale_q(t, s >= TILES)

@@ -25,7 +25,7 @@ BATCHES = TILES // BATCH
 WORDS = D // 2
 
 POW_ROUNDS = 9
-ROUNDS = 15 + POW_ROUNDS
+ROUNDS = 15 + 12 + POW_ROUNDS
 Q_ROWS_AHEAD = 3
 LAG = BATCH - 1 + ROUNDS // 2 + Q_ROWS_AHEAD
 FEED_AHEAD = 2
@@ -182,10 +182,10 @@ def tile_directnodecomphyperbolicforecaster_pa_t_kernel(
             mult, add = ALU.mult, ALU.add
 
             norms_and_rho = [
-                [
-                    lambda: vec.tensor_scalar_max(out=sq[:], in0=sums[:, :, cols], scalar1=EPS),
-                    lambda: nc.scalar.activation(out=norms[:], in_=sq[:], func=ACT.Sqrt),
-                ],
+                [lambda: vec.tensor_scalar_max(out=sq[:], in0=sums[:, :, cols], scalar1=EPS)],
+                [], [], [],
+                [lambda: nc.scalar.activation(out=norms[:], in_=sq[:], func=ACT.Sqrt)],
+                [], [],
                 [
                     lambda: vec.reciprocal(out=factors[:, 0:2, :], in_=norms[:]),
                     lambda: vec.tensor_scalar(
@@ -250,10 +250,10 @@ def tile_directnodecomphyperbolicforecaster_pa_t_kernel(
                     )
                 ],
                 [lambda: vec.reciprocal(out=neg_inv_pair[:], in_=neg_pair[:])],
-                [
-                    lambda: vec.tensor_mul(out=inv_mm[:], in0=neg_pair[:, 0, :], in1=neg_inv_pair[:, 1, :]),
-                    lambda: nc.scalar.activation(out=inv_m_norm[:], in_=inv_mm[:], func=ACT.Sqrt),
-                ],
+                [lambda: vec.tensor_mul(out=inv_mm[:], in0=neg_pair[:, 0, :], in1=neg_inv_pair[:, 1, :])],
+                [], [], [],
+                [lambda: nc.scalar.activation(out=inv_m_norm[:], in_=inv_mm[:], func=ACT.Sqrt)],
+                [], [],
             ]
             projection = [
                 [
@@ -362,7 +362,8 @@ def tile_directnodecomphyperbolicforecaster_pa_t_kernel(
                 sum_squares(acc[:], sums[:, 1, s : s + 1])
             if written(s) is not None:
                 write_tile(written(s))
-            issue_round(b, 2 * since - 1)
+            for earlier in range(b + 1):
+                issue_round(earlier, 2 * (s + 1 - (earlier + 1) * BATCH) - 1)
             if s < TILES:
                 sum_mx_times_q(acc[:], s)
                 g, j = divmod(s, GROUP)
@@ -377,7 +378,8 @@ def tile_directnodecomphyperbolicforecaster_pa_t_kernel(
                     sum_squares(x_sb[:, s + X_AHEAD, :], sums[:, 0, s + X_AHEAD : s + X_AHEAD + 1])
             if since == 0:
                 rounds[b] = coefficient_rounds(b, POW_ROUNDS + (2 * HOLD if b == BATCHES - 1 else 0))
-            issue_round(b, 2 * since)
+            for earlier in range(b + 1):
+                issue_round(earlier, 2 * (s + 1 - (earlier + 1) * BATCH))
             t = written(s + Q_ROWS_AHEAD)
             if t is not None:
                 scale_q(t, s >= TILES)

@@ -27,7 +27,8 @@ WORDS = D // 2
 POW_ROUNDS = 9
 ROUNDS = 15 + 12 + POW_ROUNDS
 Q_ROWS_AHEAD = 3
-LAG = BATCH - 1 + ROUNDS // 2 + Q_ROWS_AHEAD
+DOT_BEHIND = 1
+LAG = BATCH - 1 + DOT_BEHIND + ROUNDS // 2 + Q_ROWS_AHEAD
 FEED_AHEAD = 2
 X_AHEAD = 8
 HOLD = 4
@@ -275,10 +276,12 @@ def tile_directnodecomphyperbolicforecaster_pa_t_kernel(
 
         rounds = {}
 
-        def issue_round(b, k):
-            if b in rounds and 0 <= k < len(rounds[b]):
-                for issue in rounds[b][k]:
-                    issue()
+        def issue_rounds(s, early):
+            for b in sorted(rounds):
+                k = 2 * (s + 1 - DOT_BEHIND - (b + 1) * BATCH) - early
+                if 0 <= k < len(rounds[b]):
+                    for issue in rounds[b][k]:
+                        issue()
 
         q_rows = {}
         result = {}
@@ -353,33 +356,33 @@ def tile_directnodecomphyperbolicforecaster_pa_t_kernel(
                 return None
             return s - LAG - HOLD if s - LAG - HOLD < TILES else None
 
+        accs = {}
         for s in range(TILES + LAG + HOLD):
-            b = min((s + 1) // BATCH, BATCHES) - 1
-            since = s + 1 - (b + 1) * BATCH
             if s < TILES:
-                acc = psum_a.tile([P, D], F32, name="acc_a")
-                product(acc[:], s)
-                sum_squares(acc[:], sums[:, 1, s : s + 1])
+                accs[s] = psum_a.tile([P, D], F32, name="acc_a")
+                product(accs[s][:], s)
+                sum_squares(accs[s][:], sums[:, 1, s : s + 1])
             if written(s) is not None:
                 write_tile(written(s))
-            for earlier in range(b + 1):
-                issue_round(earlier, 2 * (s + 1 - (earlier + 1) * BATCH) - 1)
+            issue_rounds(s, 1)
+            if DOT_BEHIND <= s < TILES + DOT_BEHIND:
+                sum_mx_times_q(accs[s - DOT_BEHIND][:], s - DOT_BEHIND)
             if s < TILES:
-                sum_mx_times_q(acc[:], s)
                 g, j = divmod(s, GROUP)
+                if j == 0 and FEED_AHEAD <= g - 1 + FEED_AHEAD < GROUPS:
+                    quantise_group(g - 1 + FEED_AHEAD)
                 if g + FEED_AHEAD < GROUPS:
                     if j == 0:
                         transpose_group(g + FEED_AHEAD)
-                    elif j == GROUP - 1:
-                        quantise_group(g + FEED_AHEAD)
-                    else:
+                    elif j < GROUP - 1:
                         regroup_half(g + FEED_AHEAD, j - 1, s < LAG)
                 if s + X_AHEAD < TILES:
                     sum_squares(x_sb[:, s + X_AHEAD, :], sums[:, 0, s + X_AHEAD : s + X_AHEAD + 1])
-            if since == 0:
-                rounds[b] = coefficient_rounds(b, POW_ROUNDS + (2 * HOLD if b == BATCHES - 1 else 0))
-            for earlier in range(b + 1):
-                issue_round(earlier, 2 * (s + 1 - (earlier + 1) * BATCH))
+            started, since = divmod(s + 1 - DOT_BEHIND, BATCH)
+            if since == 0 and 1 <= started <= BATCHES:
+                last = started == BATCHES
+                rounds[started - 1] = coefficient_rounds(started - 1, POW_ROUNDS + (2 * HOLD if last else 0))
+            issue_rounds(s, 0)
             t = written(s + Q_ROWS_AHEAD)
             if t is not None:
                 scale_q(t, s >= TILES)

@@ -67,7 +67,8 @@ def tile_directnodecomphyperbolicforecaster_pa_t_kernel(
         w_words = keep.tile([P, 2 * D], U8, name="w_words", align_bytes=64)
         w_scales = keep.tile([P, D], U8, name="w_scales", align_bytes=64)
         ident = keep.tile([P, P], F32, name="ident")
-        b_all = keep.tile([P, D], BF16, name="b_all")
+        b_row = keep.tile([P, D], BF16, name="b_row")
+        ones = keep.tile([P, P], BF16, name="ones")
         q_all = keep.tile([P, D], F32, name="q_all")
         two = keep.tile([P, 1], F32, name="two")
         warm = keep.tile([P, 1], F32, name="warm")
@@ -81,6 +82,8 @@ def tile_directnodecomphyperbolicforecaster_pa_t_kernel(
         nc.vector.memset(w_scales[:].bitcast(I32), 0)
         nc.vector.memset(two[:], 2.0)
         nc.vector.memset(warm[:], 1.0)
+        nc.vector.memset(b_row[:], 0.0)
+        nc.vector.memset(ones[:], 1.0)
         nc.scalar.activation(out=warm[:], in_=warm[:], func=ACT.Sqrt)
         make_identity(nc, ident[:])
 
@@ -90,7 +93,7 @@ def tile_directnodecomphyperbolicforecaster_pa_t_kernel(
 
         for t in range(GROUP):
             nc.sync.dma_start(out=x_sb[:, t, :], in_=x_rows[:, t, :])
-        nc.scalar.dma_start(out=b_all[:], in_=b_vel.partition_broadcast(P))
+        nc.scalar.dma_start(out=b_row[0:1, :], in_=b_vel.rearrange("(o n) -> o n", o=1))
         nc.sync.dma_start(out=w_words[:].bitcast(I32), in_=W_vel_words[0].bitcast(I32))
         for quad in range(4):
             nc.sync.dma_start(
@@ -316,6 +319,8 @@ def tile_directnodecomphyperbolicforecaster_pa_t_kernel(
         b_exponent, b_power = small("b_exponent", 1), small("b_power", 1)
         b_above, b_below, b_inv_below = small("b_above", 1), small("b_below", 1), small("b_inv_below", 1)
         q_scale = small("q_scale", 1)
+        b_all = psum_a.tile([P, D], F32, name="acc_a")
+        nc.tensor.matmul(out=b_all[:], lhsT=ones[:], rhs=b_row[:], start=True, stop=True)
         sum_squares(b_all[:], b_sq[:])
         nc.vector.tensor_scalar_max(out=b_sq_clamped[:], in0=b_sq[:], scalar1=EPS)
         nc.scalar.activation(out=b_norm[:], in_=b_sq_clamped[:], func=ACT.Sqrt)

@@ -319,40 +319,43 @@ def tile_directnodecomphyperbolicforecaster_pa_t_kernel(
         b_exponent, b_power = small("b_exponent", 1), small("b_power", 1)
         b_above, b_below, b_inv_below = small("b_above", 1), small("b_below", 1), small("b_inv_below", 1)
         q_scale = small("q_scale", 1)
+        def sum_squares_on_vector(t):
+            squares = unread.tile([P, D], F32, name="by_vector")
+            nc.vector.scalar_tensor_tensor(
+                out=squares[:], in0=x_sb[:, t, :], scalar=1.0, in1=x_sb[:, t, :],
+                op0=ALU.mult, op1=ALU.mult, accum_out=sums[:, 0, t : t + 1],
+            )
+
+        transpose_group(0)
+        regroup_half(0, 0, True)
+        regroup_half(0, 1, True)
+        for t in range(3):
+            sum_squares(x_sb[:, t, :], sums[:, 0, t : t + 1])
         b_all = psum_a.tile([P, D], F32, name="acc_a")
         nc.tensor.matmul(out=b_all[:], lhsT=ones[:], rhs=b_row[:], start=True, stop=True)
         sum_squares(b_all[:], b_sq[:])
         nc.vector.tensor_scalar_max(out=b_sq_clamped[:], in0=b_sq[:], scalar1=EPS)
         nc.scalar.activation(out=b_norm[:], in_=b_sq_clamped[:], func=ACT.Sqrt)
+        quantise_group(0)
         nc.vector.tensor_scalar_mul(out=b_exponent[:], in0=b_norm[:], scalar1=TWO_LOG2E)
         nc.gpsimd.tensor_tensor(out=b_power[:], in0=two[:], in1=b_exponent[:], op=ALU.pow)
-        transpose_group(0)
-        regroup_half(0, 0, True)
-        regroup_half(0, 1, True)
-        quantise_group(0)
-        nc.vector.tensor_scalar_add(out=b_above[:], in0=b_power[:], scalar1=-1.0)
-        nc.vector.scalar_tensor_tensor(
-            out=b_below[:], in0=b_power[:], scalar=1.0, in1=b_norm[:], op0=ALU.add, op1=ALU.mult
-        )
-        nc.vector.reciprocal(out=b_inv_below[:], in_=b_below[:])
-        nc.vector.tensor_mul(out=q_scale[:], in0=b_above[:], in1=b_inv_below[:])
-        nc.vector.tensor_scalar_mul(out=q_all[:], in0=b_all[:], scalar1=q_scale[:, 0:1])
+        for t in range(3, X_AHEAD - 2):
+            sum_squares(x_sb[:, t, :], sums[:, 0, t : t + 1])
         for g in range(1, FEED_AHEAD):
             transpose_group(g)
             regroup_half(g, 0, True)
             regroup_half(g, 1, True)
+        nc.vector.tensor_scalar_add(out=b_above[:], in0=b_power[:], scalar1=-1.0)
+        nc.vector.scalar_tensor_tensor(
+            out=b_below[:], in0=b_power[:], scalar=1.0, in1=b_norm[:], op0=ALU.add, op1=ALU.mult
+        )
+        for g in range(1, FEED_AHEAD):
             quantise_group(g)
-        for t in range(X_AHEAD):
-            if t < X_AHEAD - 2:
-                sum_squares(x_sb[:, t, :], sums[:, 0, t : t + 1])
-            else:
-                squares = unread.tile([P, D], F32, name="by_vector")
-                nc.vector.scalar_tensor_tensor(
-                    out=squares[:], in0=x_sb[:, t, :], scalar=1.0, in1=x_sb[:, t, :],
-                    op0=ALU.mult, op1=ALU.mult, accum_out=sums[:, 0, t : t + 1],
-                )
-        sum_squares(q_all[:], q_sq[:])
-        nc.vector.tensor_scalar_add(out=q_sq_m1[:], in0=q_sq[:], scalar1=-1.0)
+        nc.vector.reciprocal(out=b_inv_below[:], in_=b_below[:])
+        sum_squares_on_vector(X_AHEAD - 2)
+        nc.vector.tensor_mul(out=q_scale[:], in0=b_above[:], in1=b_inv_below[:])
+        sum_squares_on_vector(X_AHEAD - 1)
+        nc.vector.tensor_scalar_mul(out=q_all[:], in0=b_all[:], scalar1=q_scale[:, 0:1])
 
         def written(s):
             if s < TILES - HOLD:
@@ -388,6 +391,9 @@ def tile_directnodecomphyperbolicforecaster_pa_t_kernel(
                 last = started == BATCHES
                 rounds[started - 1] = coefficient_rounds(started - 1, POW_ROUNDS + (2 * HOLD if last else 0))
             issue_rounds(s, 0)
+            if s == GROUP:
+                sum_squares(q_all[:], q_sq[:])
+                nc.vector.tensor_scalar_add(out=q_sq_m1[:], in0=q_sq[:], scalar1=-1.0)
             t = written(s + Q_ROWS_AHEAD)
             if t is not None:
                 scale_q(t, s >= TILES)

@@ -370,11 +370,11 @@ def tile_directnodecomphyperbolicforecaster_pa_t_kernel(
                 accs[s] = psum_a.tile([P, D], F32, name="acc_a")
                 product(accs[s][:], s)
                 sum_squares(accs[s][:], sums[:, 1, s : s + 1])
-            if written(s) is not None:
-                write_tile(written(s))
-            issue_rounds(s, 1)
             if DOT_BEHIND <= s < TILES + DOT_BEHIND:
                 sum_mx_times_q(accs[s - DOT_BEHIND][:], s - DOT_BEHIND)
+            issue_rounds(s, 1)
+            if written(s) is not None:
+                write_tile(written(s))
             if s < TILES:
                 g, j = divmod(s, GROUP)
                 if j == 0 and FEED_AHEAD <= g - 1 + FEED_AHEAD < GROUPS:
@@ -385,7 +385,10 @@ def tile_directnodecomphyperbolicforecaster_pa_t_kernel(
                     elif j < GROUP - 1:
                         regroup_half(g + FEED_AHEAD, j - 1, s < LAG)
                 if s + X_AHEAD < TILES:
-                    sum_squares(x_sb[:, s + X_AHEAD, :], sums[:, 0, s + X_AHEAD : s + X_AHEAD + 1])
+                    if s < LAG and s % 8 == 7:
+                        sum_squares_on_vector(s + X_AHEAD)
+                    else:
+                        sum_squares(x_sb[:, s + X_AHEAD, :], sums[:, 0, s + X_AHEAD : s + X_AHEAD + 1])
             started, since = divmod(s + 1 - DOT_BEHIND, BATCH)
             if since == 0 and 1 <= started <= BATCHES:
                 last = started == BATCHES

@@ -366,6 +366,11 @@ def tile_directnodecomphyperbolicforecaster_pa_t_kernel(
 
         accs = {}
         for s in range(TILES + LAG + HOLD):
+            if s + X_AHEAD < TILES:
+                if s < LAG and s % 8 == 7:
+                    sum_squares_on_vector(s + X_AHEAD)
+                else:
+                    sum_squares(x_sb[:, s + X_AHEAD, :], sums[:, 0, s + X_AHEAD : s + X_AHEAD + 1])
             if s < TILES:
                 accs[s] = psum_a.tile([P, D], F32, name="acc_a")
                 product(accs[s][:], s)
@@ -384,11 +389,6 @@ def tile_directnodecomphyperbolicforecaster_pa_t_kernel(
                         transpose_group(g + FEED_AHEAD)
                     elif j < GROUP - 1:
                         regroup_half(g + FEED_AHEAD, j - 1, s < LAG)
-                if s + X_AHEAD < TILES:
-                    if s < LAG and s % 8 == 7:
-                        sum_squares_on_vector(s + X_AHEAD)
-                    else:
-                        sum_squares(x_sb[:, s + X_AHEAD, :], sums[:, 0, s + X_AHEAD : s + X_AHEAD + 1])
             started, since = divmod(s + 1 - DOT_BEHIND, BATCH)
             if since == 0 and 1 <= started <= BATCHES:
                 last = started == BATCHES

@@ -32,6 +32,9 @@ LAG = BATCH - 1 + DOT_BEHIND + ROUNDS // 2 + Q_ROWS_AHEAD
 FEED_AHEAD = 2
 X_AHEAD = 8
 HOLD = 4
+GRAM_FIRST = 8
+GRAM_TILES = 24
+GRAM_AHEAD = 4
 
 EPS = 1e-15
 MAXN = 1.0 - 1e-5
@@ -357,6 +360,25 @@ def tile_directnodecomphyperbolicforecaster_pa_t_kernel(
         sum_squares_on_vector(X_AHEAD - 1)
         nc.vector.tensor_scalar_mul(out=q_all[:], in0=b_all[:], scalar1=q_scale[:, 0:1])
 
+        def by_gram(t):
+            return GRAM_FIRST <= t < GRAM_FIRST + GRAM_TILES
+
+        grams = {}
+
+        def gram(t):
+            g, j = divmod(t, GROUP)
+            grams[t] = psum_b.tile([P, P], F32, name="acc_b")
+            for c in range(PACK):
+                x_t = regrouped[g][:, j, :, c]
+                nc.tensor.matmul(out=grams[t][:], lhsT=x_t, rhs=x_t, start=(c == 0), stop=(c == PACK - 1))
+
+        def sum_diagonal(t):
+            masked = unread.tile([P, D], F32, name="by_vector")
+            nc.vector.scalar_tensor_tensor(
+                out=masked[:, 0:P], in0=grams[t][:], scalar=1.0, in1=ident[:], op0=ALU.mult, op1=ALU.mult,
+                accum_out=sums[:, 0, t : t + 1],
+            )
+
         def written(s):
             if s < TILES - HOLD:
                 return s - LAG if s >= LAG else None
@@ -366,7 +388,7 @@ def tile_directnodecomphyperbolicforecaster_pa_t_kernel(
 
         accs = {}
         for s in range(TILES + LAG + HOLD):
-            if s + X_AHEAD < TILES:
+            if s + X_AHEAD < TILES and not by_gram(s + X_AHEAD):
                 if s < LAG and s % 8 == 7:
                     sum_squares_on_vector(s + X_AHEAD)
                 else:
@@ -375,8 +397,12 @@ def tile_directnodecomphyperbolicforecaster_pa_t_kernel(
                 accs[s] = psum_a.tile([P, D], F32, name="acc_a")
                 product(accs[s][:], s)
                 sum_squares(accs[s][:], sums[:, 1, s : s + 1])
+            if by_gram(s + GRAM_AHEAD):
+                gram(s + GRAM_AHEAD)
             if DOT_BEHIND <= s < TILES + DOT_BEHIND:
                 sum_mx_times_q(accs[s - DOT_BEHIND][:], s - DOT_BEHIND)
+            if by_gram(s + GRAM_AHEAD - 1):
+                sum_diagonal(s + GRAM_AHEAD - 1)
             issue_rounds(s, 1)
             if written(s) is not None:
                 write_tile(written(s))
@@ -388,7 +414,7 @@ def tile_directnodecomphyperbolicforecaster_pa_t_kernel(
                     if j == 0:
                         transpose_group(g + FEED_AHEAD)
                     elif j < GROUP - 1:
-                        regroup_half(g + FEED_AHEAD, j - 1, s < LAG)
+                        regroup_half(g + FEED_AHEAD, j - 1, s < LAG and not by_gram(s + X_AHEAD))
             started, since = divmod(s + 1 - DOT_BEHIND, BATCH)
             if since == 0 and 1 <= started <= BATCHES:
                 last = started == BATCHES

@@ -24,9 +24,10 @@ BATCH = 16
 BATCHES = TILES // BATCH
 WORDS = D // 2
 
-POW_ROUNDS = 9
-ROUNDS = 15 + 12 + POW_ROUNDS
+POW_ROUNDS = 10
+ROUNDS = 14 + 5 + POW_ROUNDS
 Q_ROWS_AHEAD = 3
+Q_ROWS_MOST = 7
 DOT_BEHIND = 1
 LAG = BATCH - 1 + DOT_BEHIND + ROUNDS // 2 + Q_ROWS_AHEAD
 FEED_AHEAD = 2
@@ -56,11 +57,9 @@ def tile_directnodecomphyperbolicforecaster_pa_t_kernel(
         stage = ctx.enter_context(tc.tile_pool(name="stage", bufs=3))
         unread = ctx.enter_context(tc.tile_pool(name="unread", bufs=3))
         chain = ctx.enter_context(tc.tile_pool(name="chain", bufs=2))
-        bias_rows = ctx.enter_context(tc.tile_pool(name="bias_rows", bufs=Q_ROWS_AHEAD + 2))
+        bias_rows = ctx.enter_context(tc.tile_pool(name="bias_rows", bufs=Q_ROWS_MOST + 2))
         results = ctx.enter_context(tc.tile_pool(name="results", bufs=3))
-        psum_t = ctx.enter_context(tc.psum_pool(name="psum_t", bufs=2))
-        psum_a = ctx.enter_context(tc.psum_pool(name="psum_a", bufs=3))
-        psum_b = ctx.enter_context(tc.psum_pool(name="psum_b", bufs=3))
+        psum = ctx.enter_context(tc.psum_pool(name="psum", bufs=8))
         ctx.enter_context(tc.manual_schedule())
 
         x_sb = keep.tile([P, TILES, D], BF16, name="x_sb")
@@ -76,9 +75,8 @@ def tile_directnodecomphyperbolicforecaster_pa_t_kernel(
         two = keep.tile([P, 1], F32, name="two")
         warm = keep.tile([P, 1], F32, name="warm")
         sums = keep.tile([P, 2, TILES], F32, name="sums")
-        mx_dot_q = keep.tile([P, TILES], F32, name="mx_dot_q")
-        coef_mx = keep.tile([P, TILES], F32, name="coef_mx")
-        coef_q = keep.tile([P, TILES], F32, name="coef_q")
+        norms_dot = keep.tile([P, BATCHES, 3, BATCH], F32, name="norms_dot")
+        coefs = keep.tile([P, BATCHES, 2, BATCH], F32, name="coefs")
         q_sq = keep.tile([P, 1], F32, name="q_sq")
         q_sq_m1 = keep.tile([P, 1], F32, name="q_sq_m1")
 
@@ -115,7 +113,7 @@ def tile_directnodecomphyperbolicforecaster_pa_t_kernel(
         def transpose_group(g):
             transposed[g] = []
             for half in range(GROUP // 2):
-                xt = psum_t.tile([P, 2, 2, P], F32, name="xt")
+                xt = psum.tile([P, 2, 2, P], F32, name="bank")
                 for j in range(2):
                     t = g * GROUP + 2 * half + j
                     for u in range(2):
@@ -160,41 +158,38 @@ def tile_directnodecomphyperbolicforecaster_pa_t_kernel(
         def sum_mx_times_q(acc, t):
             products = unread.tile([P, D], F32, name="by_vector")
             nc.vector.scalar_tensor_tensor(
-                out=products[:], in0=acc, scalar=1.0, in1=q_all[:], op0=ALU.mult, op1=ALU.mult,
-                accum_out=mx_dot_q[:, t : t + 1],
+                out=products[:], in0=acc, scalar=2.0, in1=q_all[:], op0=ALU.mult, op1=ALU.mult,
+                accum_out=norms_dot[:, t // BATCH, 2, t % BATCH : t % BATCH + 1],
             )
 
         def coefficient_rounds(b, pow_rounds):
             cols = slice(b * BATCH, (b + 1) * BATCH)
             vec = nc.vector
             sq = chain.tile([P, 2, BATCH], F32, name="sq")
-            norms = chain.tile([P, 2, BATCH], F32, name="norms")
-            xn, mxn = norms[:, 0, :], norms[:, 1, :]
+            norms = norms_dot[:, b, 0:2, :]
+            xn = norms_dot[:, b, 0, :]
             factors = chain.tile([P, 4, BATCH], F32, name="factors")
-            inv_xn, inv_mxn, dot_over_mxn, neg_tanh = (
-                factors[:, 0, :], factors[:, 1, :], factors[:, 2, :], factors[:, 3, :]
-            )
+            kappa = factors[:, 2, :]
+            neg_tanh = factors[:, 2, :]
             products = chain.tile([P, 3, BATCH], F32, name="products")
-            neg_a, neg_pq, pp = products[:, 0, :], products[:, 1, :], products[:, 2, :]
+            neg_a, pp = products[:, 0, :], products[:, 1, :]
+            terms = chain.tile([P, 3, BATCH], F32, name="terms")
+            one_2pq = terms[:, 2, :]
             c_minus_one, inv_c_minus_one = small("c_minus_one"), small("inv_c_minus_one")
-            rho, kappa = small("rho"), small("kappa")
+            rho = small("rho")
             power, power_plus_one, inverse = small("power"), small("power_plus_one"), small("inverse")
-            one_2pq, neg_c_p_a = small("one_2pq"), small("neg_c_p_a")
-            pair = chain.tile([P, 2, BATCH], F32, name="pair")
-            neg_pair = chain.tile([P, 2, BATCH], F32, name="neg_pair")
-            neg_inv_pair = chain.tile([P, 2, BATCH], F32, name="neg_inv_pair")
-            neg_inv_den = neg_inv_pair[:, 0, :]
-            inv_mm, inv_m_norm = small("inv_mm"), small("inv_m_norm")
-            neg_scaled, neg_common = small("neg_scaled"), small("neg_common")
+            den, den_clamped, inv_den = small("den"), small("den_clamped"), small("inv_den")
+            mm_den, excess, neg_shrink = small("mm_den"), small("excess"), small("neg_shrink")
+            neg_common = chain.tile([P, 1, BATCH], F32, name="neg_common")
             mult, add = ALU.mult, ALU.add
 
             norms_and_rho = [
                 [lambda: vec.tensor_scalar_max(out=sq[:], in0=sums[:, :, cols], scalar1=EPS)],
                 [], [], [],
-                [lambda: nc.scalar.activation(out=norms[:], in_=sq[:], func=ACT.Sqrt)],
+                [lambda: nc.scalar.activation(out=norms, in_=sq[:], func=ACT.Sqrt)],
                 [], [],
                 [
-                    lambda: vec.reciprocal(out=factors[:, 0:2, :], in_=norms[:]),
+                    lambda: vec.reciprocal(out=factors[:, 0:2, :], in_=norms),
                     lambda: vec.tensor_scalar(
                         out=c_minus_one[:], in0=xn, scalar1=CLIP, scalar2=1.0,
                         op0=ALU.min, op1=ALU.subtract,
@@ -202,16 +197,13 @@ def tile_directnodecomphyperbolicforecaster_pa_t_kernel(
                 ],
                 [
                     lambda: vec.reciprocal(out=inv_c_minus_one[:], in_=c_minus_one[:]),
-                    lambda: vec.tensor_mul(out=kappa[:], in0=mxn, in1=inv_xn),
-                    lambda: vec.tensor_mul(out=dot_over_mxn, in0=mx_dot_q[:, cols], in1=inv_mxn),
-                ],
-                [
-                    lambda: vec.tensor_scalar(
+                    lambda: vec.tensor_mul(
+                        out=factors[:, 2:4, :], in0=norms_dot[:, b, 1:3, :], in1=factors[:, 0:2, :]
+                    ),
+                    lambda: nc.gpsimd.tensor_scalar(
                         out=rho[:], in0=inv_c_minus_one[:], scalar1=-2.0, scalar2=-1.0, op0=mult, op1=add
                     ),
-                    lambda: nc.gpsimd.tensor_tensor(
-                        out=power[:], in0=rho[:], in1=kappa[:], op=ALU.pow
-                    ),
+                    lambda: nc.gpsimd.tensor_tensor(out=power[:], in0=rho[:], in1=kappa, op=ALU.pow),
                     lambda: nc.gpsimd.tensor_scalar(
                         out=power_plus_one[:], in0=power[:], scalar1=1.0, scalar2=1.0,
                         op0=add, op1=mult,
@@ -229,53 +221,53 @@ def tile_directnodecomphyperbolicforecaster_pa_t_kernel(
                 [
                     lambda: vec.tensor_mul(
                         out=products[:], in0=factors[:, 1:4, :],
-                        in1=factors[:, 3:4, :].to_broadcast([P, 3, BATCH]),
+                        in1=factors[:, 2:3, :].to_broadcast([P, 3, BATCH]),
                     )
                 ],
                 [
                     lambda: vec.tensor_scalar(
-                        out=one_2pq[:], in0=neg_pq, scalar1=-2.0, scalar2=1.0, op0=mult, op1=add
-                    )
-                ],
-                [
-                    lambda: vec.scalar_tensor_tensor(
-                        out=pair[:, 0, :], in0=pp, scalar=q_sq[:, 0:1], in1=one_2pq[:],
+                        out=terms[:, 1:3, :], in0=products[:, 1:3, :], scalar1=-1.0, scalar2=1.0,
                         op0=mult, op1=add,
-                    ),
-                    lambda: vec.scalar_tensor_tensor(
-                        out=pair[:, 1, :], in0=pp, scalar=q_sq_m1[:, 0:1], in1=one_2pq[:],
-                        op0=add, op1=add,
-                    ),
-                    lambda: vec.scalar_tensor_tensor(
-                        out=neg_c_p_a[:], in0=one_2pq[:], scalar=q_sq[:, 0:1], in1=neg_a,
-                        op0=add, op1=mult,
-                    ),
-                ],
-                [
-                    lambda: vec.tensor_scalar(
-                        out=neg_pair[:], in0=pair[:], scalar1=EPS, scalar2=-1.0, op0=ALU.max, op1=mult
                     )
                 ],
-                [lambda: vec.reciprocal(out=neg_inv_pair[:], in_=neg_pair[:])],
-                [lambda: vec.tensor_mul(out=inv_mm[:], in0=neg_pair[:, 0, :], in1=neg_inv_pair[:, 1, :])],
-                [], [], [],
-                [lambda: nc.scalar.activation(out=inv_m_norm[:], in_=inv_mm[:], func=ACT.Sqrt)],
-                [], [],
+                [
+                    lambda: vec.scalar_tensor_tensor(
+                        out=den[:], in0=pp, scalar=q_sq[:, 0:1], in1=one_2pq, op0=mult, op1=add
+                    ),
+                    lambda: vec.scalar_tensor_tensor(
+                        out=mm_den[:], in0=pp, scalar=q_sq_m1[:, 0:1], in1=one_2pq, op0=add, op1=add
+                    ),
+                    lambda: vec.scalar_tensor_tensor(
+                        out=terms[:, 0, :], in0=one_2pq, scalar=q_sq[:, 0:1], in1=neg_a, op0=add, op1=mult
+                    ),
+                ],
             ]
             projection = [
+                [lambda: vec.tensor_scalar_max(out=den_clamped[:], in0=den[:], scalar1=EPS)],
+                [
+                    lambda: vec.reciprocal(out=inv_den[:], in_=den_clamped[:]),
+                    lambda: vec.scalar_tensor_tensor(
+                        out=excess[:], in0=mm_den[:], scalar=-1.0 / 3.0, in1=den_clamped[:],
+                        op0=mult, op1=add,
+                    ),
+                ],
                 [
                     lambda: vec.scalar_tensor_tensor(
-                        out=neg_scaled[:], in0=inv_m_norm[:], scalar=MAXN, in1=neg_inv_den,
+                        out=neg_shrink[:], in0=excess[:], scalar=-1.5 * MAXN, in1=inv_den[:],
                         op0=mult, op1=mult,
                     )
                 ],
-                [lambda: vec.tensor_max(out=neg_common[:], in0=neg_scaled[:], in1=neg_inv_den)],
                 [
                     lambda: vec.scalar_tensor_tensor(
-                        out=coef_q[:, cols], in0=pp, scalar=1.0, in1=neg_common[:],
-                        op0=ALU.subtract, op1=mult,
-                    ),
-                    lambda: vec.tensor_mul(out=coef_mx[:, cols], in0=neg_c_p_a[:], in1=neg_common[:]),
+                        out=neg_common[:, 0, :], in0=neg_shrink[:], scalar=-1.0, in1=inv_den[:],
+                        op0=ALU.max, op1=mult,
+                    )
+                ],
+                [
+                    lambda: vec.tensor_mul(
+                        out=coefs[:, b, :, :], in0=terms[:, 0:2, :],
+                        in1=neg_common[:].to_broadcast([P, 2, BATCH]),
+                    )
                 ],
             ]
             return norms_and_rho + while_gpsimd_works + moebius + projection
@@ -296,11 +288,13 @@ def tile_directnodecomphyperbolicforecaster_pa_t_kernel(
             q_rows[t] = bias_rows.tile([P, D], F32, name="q_row")
             if on_scalar:
                 nc.scalar.activation(
-                    out=q_rows[t][:], in_=q_all[:], func=ACT.Copy, scale=coef_q[:, t : t + 1]
+                    out=q_rows[t][:], in_=q_all[:], func=ACT.Copy,
+                    scale=coefs[:, t // BATCH, 1, t % BATCH : t % BATCH + 1],
                 )
             else:
                 nc.gpsimd.tensor_scalar(
-                    out=q_rows[t][:], in0=q_all[:], scalar1=coef_q[:, t : t + 1], scalar2=0.0,
+                    out=q_rows[t][:], in0=q_all[:],
+                    scalar1=coefs[:, t // BATCH, 1, t % BATCH : t % BATCH + 1], scalar2=0.0,
                     op0=ALU.mult, op1=ALU.add,
                 )
 
@@ -308,11 +302,12 @@ def tile_directnodecomphyperbolicforecaster_pa_t_kernel(
             g, j = divmod(t, GROUP)
             if j == 0:
                 result[g] = results.tile([P, GROUP, D], F32, name="result")
-            acc_b = psum_b.tile([P, D], F32, name="acc_b")
+            acc_b = psum.tile([P, D], F32, name="bank")
             product(acc_b[:], t)
             nc.vector.scalar_tensor_tensor(
-                out=result[g][:, j, :], in0=acc_b[:], scalar=coef_mx[:, t : t + 1], in1=q_rows[t][:],
-                op0=ALU.mult, op1=ALU.add,
+                out=result[g][:, j, :], in0=acc_b[:],
+                scalar=coefs[:, t // BATCH, 0, t % BATCH : t % BATCH + 1], in1=q_rows[t][:],
+                op0=ALU.mult, op1=ALU.subtract,
             )
             if j == GROUP - 1:
                 tiles = slice(g * GROUP, (g + 1) * GROUP)
@@ -334,7 +329,7 @@ def tile_directnodecomphyperbolicforecaster_pa_t_kernel(
         regroup_half(0, 1, True)
         for t in range(3):
             sum_squares(x_sb[:, t, :], sums[:, 0, t : t + 1])
-        b_all = psum_a.tile([P, D], F32, name="acc_a")
+        b_all = psum.tile([P, D], F32, name="bank")
         nc.tensor.matmul(out=b_all[:], lhsT=ones[:], rhs=b_row[:], start=True, stop=True)
         sum_squares(b_all[:], b_sq[:])
         nc.vector.tensor_scalar_max(out=b_sq_clamped[:], in0=b_sq[:], scalar1=EPS)
@@ -367,7 +362,7 @@ def tile_directnodecomphyperbolicforecaster_pa_t_kernel(
 
         def gram(t):
             g, j = divmod(t, GROUP)
-            grams[t] = psum_b.tile([P, P], F32, name="acc_b")
+            grams[t] = psum.tile([P, P], F32, name="bank")
             for c in range(PACK):
                 x_t = regrouped[g][:, j, :, c]
                 nc.tensor.matmul(out=grams[t][:], lhsT=x_t, rhs=x_t, start=(c == 0), stop=(c == PACK - 1))
@@ -386,6 +381,12 @@ def tile_directnodecomphyperbolicforecaster_pa_t_kernel(
                 return None
             return s - LAG - HOLD if s - LAG - HOLD < TILES else None
 
+        def slot_of(t):
+            return t + LAG if t + LAG < TILES - HOLD else t + LAG + HOLD
+
+        def known(b):
+            return (b + 1) * BATCH - 1 + DOT_BEHIND + ROUNDS // 2 + (HOLD if b == BATCHES - 1 else 0)
+
         accs = {}
         for s in range(TILES + LAG + HOLD):
             if s + X_AHEAD < TILES and not by_gram(s + X_AHEAD):
@@ -394,7 +395,7 @@ def tile_directnodecomphyperbolicforecaster_pa_t_kernel(
                 else:
                     sum_squares(x_sb[:, s + X_AHEAD, :], sums[:, 0, s + X_AHEAD : s + X_AHEAD + 1])
             if s < TILES:
-                accs[s] = psum_a.tile([P, D], F32, name="acc_a")
+                accs[s] = psum.tile([P, D], F32, name="bank")
                 product(accs[s][:], s)
                 sum_squares(accs[s][:], sums[:, 1, s : s + 1])
             if by_gram(s + GRAM_AHEAD):
@@ -423,6 +424,6 @@ def tile_directnodecomphyperbolicforecaster_pa_t_kernel(
             if s == GROUP:
                 sum_squares(q_all[:], q_sq[:])
                 nc.vector.tensor_scalar_add(out=q_sq_m1[:], in0=q_sq[:], scalar1=-1.0)
-            t = written(s + Q_ROWS_AHEAD)
-            if t is not None:
-                scale_q(t, s >= TILES)
+            for t in range(TILES):
+                if t not in q_rows and known(t // BATCH) <= s and slot_of(t) <= s + Q_ROWS_MOST:
+                    scale_q(t, s >= TILES)

@@ -95,13 +95,14 @@ def tile_directnodecomphyperbolicforecaster_pa_t_kernel(
         for t in range(GROUP):
             nc.sync.dma_start(out=x_sb[:, t, :], in_=x_rows[:, t, :])
         nc.scalar.dma_start(out=b_row[0:1, :], in_=b_vel.rearrange("(o n) -> o n", o=1))
+        load_group(1)
         nc.sync.dma_start(out=w_words[:].bitcast(I32), in_=W_vel_words[0].bitcast(I32))
         for quad in range(4):
             nc.sync.dma_start(
                 out=w_scales[32 * quad : 32 * quad + 4, :].bitcast(I32),
                 in_=W_vel_scales[0, 4 * quad : 4 * quad + 4, :].bitcast(I32),
             )
-        for g in range(1, GROUPS):
+        for g in range(2, GROUPS):
             load_group(g)
 
         def small(name, width=BATCH):
@@ -327,32 +328,28 @@ def tile_directnodecomphyperbolicforecaster_pa_t_kernel(
         transpose_group(0)
         regroup_half(0, 0, True)
         regroup_half(0, 1, True)
-        for t in range(3):
+        for t in range(X_AHEAD - 2):
             sum_squares(x_sb[:, t, :], sums[:, 0, t : t + 1])
         b_all = psum.tile([P, D], F32, name="bank")
         nc.tensor.matmul(out=b_all[:], lhsT=ones[:], rhs=b_row[:], start=True, stop=True)
         sum_squares(b_all[:], b_sq[:])
+        sum_squares_on_vector(X_AHEAD - 2)
+        quantise_group(0)
         nc.vector.tensor_scalar_max(out=b_sq_clamped[:], in0=b_sq[:], scalar1=EPS)
         nc.scalar.activation(out=b_norm[:], in_=b_sq_clamped[:], func=ACT.Sqrt)
-        quantise_group(0)
+        transpose_group(1)
+        regroup_half(1, 0, True)
         nc.vector.tensor_scalar_mul(out=b_exponent[:], in0=b_norm[:], scalar1=TWO_LOG2E)
         nc.gpsimd.tensor_tensor(out=b_power[:], in0=two[:], in1=b_exponent[:], op=ALU.pow)
-        for t in range(3, X_AHEAD - 2):
-            sum_squares(x_sb[:, t, :], sums[:, 0, t : t + 1])
-        for g in range(1, FEED_AHEAD):
-            transpose_group(g)
-            regroup_half(g, 0, True)
-            regroup_half(g, 1, True)
+        regroup_half(1, 1, True)
+        sum_squares_on_vector(X_AHEAD - 1)
         nc.vector.tensor_scalar_add(out=b_above[:], in0=b_power[:], scalar1=-1.0)
         nc.vector.scalar_tensor_tensor(
             out=b_below[:], in0=b_power[:], scalar=1.0, in1=b_norm[:], op0=ALU.add, op1=ALU.mult
         )
-        for g in range(1, FEED_AHEAD):
-            quantise_group(g)
+        quantise_group(1)
         nc.vector.reciprocal(out=b_inv_below[:], in_=b_below[:])
-        sum_squares_on_vector(X_AHEAD - 2)
         nc.vector.tensor_mul(out=q_scale[:], in0=b_above[:], in1=b_inv_below[:])
-        sum_squares_on_vector(X_AHEAD - 1)
         nc.vector.tensor_scalar_mul(out=q_all[:], in0=b_all[:], scalar1=q_scale[:, 0:1])
 
         def by_gram(t):

from contextlib import ExitStack

import concourse.mybir as mybir
from concourse.masks import make_identity

F32 = mybir.dt.float32
BF16 = mybir.dt.bfloat16
I32 = mybir.dt.int32
U32 = mybir.dt.uint32
U8 = mybir.dt.uint8
FP8X4 = mybir.dt.float8_e4m3fn_x4
FP4X4 = mybir.dt.float4_e2m1fn_x4
ALU = mybir.AluOpType
ACT = mybir.ActivationFunctionType

P = 128
PACK = 4
ROWS = 8192
D = 512
TILES = ROWS // P
GROUP = 4
GROUPS = TILES // GROUP
BATCH = 16
BATCHES = TILES // BATCH
WORDS = D // 2

POW_ROUNDS = 10
ROUNDS = 14 + 5 + POW_ROUNDS
Q_ROWS_AHEAD = 3
Q_ROWS_MOST = 7
DOT_BEHIND = 1
LAG = BATCH - 1 + DOT_BEHIND + ROUNDS // 2 + Q_ROWS_AHEAD
FEED_AHEAD = 2
X_AHEAD = 8
HOLD = 4
GRAM_FIRST = 8
GRAM_TILES = 24
GRAM_AHEAD = 4

EPS = 1e-15
MAXN = 1.0 - 1e-5
CLIP = 1.0 - 1e-7
TWO_LOG2E = 2.8853900817779268

FLOPS = 2 * ROWS * D * D


def tile_directnodecomphyperbolicforecaster_pa_t_kernel(
    tc, v_init, W_vel_words, W_vel_scales, b_vel, out
):
    nc = tc.nc
    x_rows = v_init.rearrange("(p t) k -> p t k", t=TILES)
    out_rows = out.rearrange("(p t) n -> p t n", t=TILES)

    with ExitStack() as ctx:
        keep = ctx.enter_context(tc.tile_pool(name="keep", bufs=1))
        stage = ctx.enter_context(tc.tile_pool(name="stage", bufs=3))
        unread = ctx.enter_context(tc.tile_pool(name="unread", bufs=3))
        chain = ctx.enter_context(tc.tile_pool(name="chain", bufs=2))
        bias_rows = ctx.enter_context(tc.tile_pool(name="bias_rows", bufs=Q_ROWS_MOST + 2))
        results = ctx.enter_context(tc.tile_pool(name="results", bufs=3))
        psum = ctx.enter_context(tc.psum_pool(name="psum", bufs=8))
        ctx.enter_context(tc.manual_schedule())

        x_sb = keep.tile([P, TILES, D], BF16, name="x_sb")
        x_words = x_sb[:].bitcast(F32)
        x_codes = keep.tile([P, TILES * P], U32, name="x_codes", align_bytes=64)
        x_scales = keep.tile([P, TILES * P], U8, name="x_scales", align_bytes=64)
        w_words = keep.tile([P, 2 * D], U8, name="w_words", align_bytes=64)
        w_scales = keep.tile([P, D], U8, name="w_scales", align_bytes=64)
        ident = keep.tile([P, P], F32, name="ident")
        b_row = keep.tile([P, D], BF16, name="b_row")
        ones = keep.tile([P, P], BF16, name="ones")
        q_all = keep.tile([P, D], F32, name="q_all")
        two = keep.tile([P, 1], F32, name="two")
        warm = keep.tile([P, 1], F32, name="warm")
        sums = keep.tile([P, 2, TILES], F32, name="sums")
        norms_dot = keep.tile([P, BATCHES, 3, BATCH], F32, name="norms_dot")
        coefs = keep.tile([P, BATCHES, 2, BATCH], F32, name="coefs")
        q_sq = keep.tile([P, 1], F32, name="q_sq")
        q_sq_m1 = keep.tile([P, 1], F32, name="q_sq_m1")

        nc.vector.memset(w_scales[:].bitcast(I32), 0)
        nc.vector.memset(two[:], 2.0)
        nc.vector.memset(warm[:], 1.0)
        nc.vector.memset(b_row[:], 0.0)
        nc.vector.memset(ones[:], 1.0)
        nc.scalar.activation(out=warm[:], in_=warm[:], func=ACT.Sqrt)
        make_identity(nc, ident[:])

        def load_group(g):
            tiles = slice(g * GROUP, (g + 1) * GROUP)
            nc.sync.dma_start(out=x_sb[:, tiles, :], in_=x_rows[:, tiles, :])

        for t in range(GROUP):
            nc.sync.dma_start(out=x_sb[:, t, :], in_=x_rows[:, t, :])
        nc.scalar.dma_start(out=b_row[0:1, :], in_=b_vel.rearrange("(o n) -> o n", o=1))
        load_group(1)
        nc.sync.dma_start(out=w_words[:].bitcast(I32), in_=W_vel_words[0].bitcast(I32))
        for quad in range(4):
            nc.sync.dma_start(
                out=w_scales[32 * quad : 32 * quad + 4, :].bitcast(I32),
                in_=W_vel_scales[0, 4 * quad : 4 * quad + 4, :].bitcast(I32),
            )
        for g in range(2, GROUPS):
            load_group(g)

        def small(name, width=BATCH):
            return chain.tile([P, width], F32, name=name)

        transposed = {}
        regrouped = {}

        def transpose_group(g):
            transposed[g] = []
            for half in range(GROUP // 2):
                xt = psum.tile([P, 2, 2, P], F32, name="bank")
                for j in range(2):
                    t = g * GROUP + 2 * half + j
                    for u in range(2):
                        nc.tensor.transpose(xt[:, j, u, :], x_words[:, t, u:WORDS:2], ident[:])
                transposed[g].append(xt)

        def regroup_half(g, half, on_vector):
            if half == 0:
                regrouped[g] = stage.tile([P, GROUP, P, PACK], BF16, name="grouped", align_bytes=64)
            grouped_words = regrouped[g][:].bitcast(F32)
            dst = grouped_words[:, 2 * half : 2 * half + 2, :, :]
            src = transposed[g][half][:].rearrange("p j u r -> p j r u")
            if on_vector:
                nc.vector.tensor_copy(out=dst, in_=src)
            else:
                nc.scalar.copy(out=dst, in_=src)

        def quantise_group(g):
            cols = slice(g * GROUP * P, (g + 1) * GROUP * P)
            nc.vector.quantize_mx(
                out=x_codes[:, cols].bitcast(FP8X4),
                scales=x_scales[:, cols],
                in_=regrouped[g][:].rearrange("p j r t -> p (j r t)"),
            )

        def product(acc, t):
            rows = slice(t * P, (t + 1) * P)
            nc.tensor.matmul_mx(
                out=acc,
                lhsT=x_codes[:, rows].bitcast(FP8X4),
                lhsT_scale=x_scales[:, rows],
                rhs=w_words[:].bitcast(FP4X4),
                rhs_scale=w_scales[:],
                start=True,
                stop=True,
            )

        def sum_squares(values, total):
            squares = unread.tile([P, D], F32, name="by_scalar")
            nc.scalar.activation(out=squares[:], in_=values, func=ACT.Square, accum_out=total)

        def sum_mx_times_q(acc, t):
            products = unread.tile([P, D], F32, name="by_vector")
            nc.vector.scalar_tensor_tensor(
                out=products[:], in0=acc, scalar=2.0, in1=q_all[:], op0=ALU.mult, op1=ALU.mult,
                accum_out=norms_dot[:, t // BATCH, 2, t % BATCH : t % BATCH + 1],
            )

        def coefficient_rounds(b, pow_rounds):
            cols = slice(b * BATCH, (b + 1) * BATCH)
            vec = nc.vector
            sq = chain.tile([P, 2, BATCH], F32, name="sq")
            norms = norms_dot[:, b, 0:2, :]
            xn = norms_dot[:, b, 0, :]
            factors = chain.tile([P, 4, BATCH], F32, name="factors")
            kappa = factors[:, 2, :]
            neg_tanh = factors[:, 2, :]
            products = chain.tile([P, 3, BATCH], F32, name="products")
            neg_a, pp = products[:, 0, :], products[:, 1, :]
            terms = chain.tile([P, 3, BATCH], F32, name="terms")
            one_2pq = terms[:, 2, :]
            c_minus_one, inv_c_minus_one = small("c_minus_one"), small("inv_c_minus_one")
            rho = small("rho")
            power, power_plus_one, inverse = small("power"), small("power_plus_one"), small("inverse")
            den, den_clamped, inv_den = small("den"), small("den_clamped"), small("inv_den")
            mm_den, excess, neg_shrink = small("mm_den"), small("excess"), small("neg_shrink")
            neg_common = chain.tile([P, 1, BATCH], F32, name="neg_common")
            mult, add = ALU.mult, ALU.add

            norms_and_rho = [
                [lambda: vec.tensor_scalar_max(out=sq[:], in0=sums[:, :, cols], scalar1=EPS)],
                [], [], [],
                [lambda: nc.scalar.activation(out=norms, in_=sq[:], func=ACT.Sqrt)],
                [], [],
                [
                    lambda: vec.reciprocal(out=factors[:, 0:2, :], in_=norms),
                    lambda: vec.tensor_scalar(
                        out=c_minus_one[:], in0=xn, scalar1=CLIP, scalar2=1.0,
                        op0=ALU.min, op1=ALU.subtract,
                    ),
                ],
                [
                    lambda: vec.reciprocal(out=inv_c_minus_one[:], in_=c_minus_one[:]),
                    lambda: vec.tensor_mul(
                        out=factors[:, 2:4, :], in0=norms_dot[:, b, 1:3, :], in1=factors[:, 0:2, :]
                    ),
                    lambda: nc.gpsimd.tensor_scalar(
                        out=rho[:], in0=inv_c_minus_one[:], scalar1=-2.0, scalar2=-1.0, op0=mult, op1=add
                    ),
                    lambda: nc.gpsimd.tensor_tensor(out=power[:], in0=rho[:], in1=kappa, op=ALU.pow),
                    lambda: nc.gpsimd.tensor_scalar(
                        out=power_plus_one[:], in0=power[:], scalar1=1.0, scalar2=1.0,
                        op0=add, op1=mult,
                    ),
                ],
            ]
            while_gpsimd_works = [[] for i in range(pow_rounds)]
            moebius = [
                [lambda: vec.reciprocal(out=inverse[:], in_=power_plus_one[:])],
                [
                    lambda: vec.tensor_scalar(
                        out=neg_tanh, in0=inverse[:], scalar1=2.0, scalar2=-1.0, op0=mult, op1=add
                    )
                ],
                [
                    lambda: vec.tensor_mul(
                        out=products[:], in0=factors[:, 1:4, :],
                        in1=factors[:, 2:3, :].to_broadcast([P, 3, BATCH]),
                    )
                ],
                [
                    lambda: vec.tensor_scalar(
                        out=terms[:, 1:3, :], in0=products[:, 1:3, :], scalar1=-1.0, scalar2=1.0,
                        op0=mult, op1=add,
                    )
                ],
                [
                    lambda: vec.scalar_tensor_tensor(
                        out=den[:], in0=pp, scalar=q_sq[:, 0:1], in1=one_2pq, op0=mult, op1=add
                    ),
                    lambda: vec.scalar_tensor_tensor(
                        out=mm_den[:], in0=pp, scalar=q_sq_m1[:, 0:1], in1=one_2pq, op0=add, op1=add
                    ),
                    lambda: vec.scalar_tensor_tensor(
                        out=terms[:, 0, :], in0=one_2pq, scalar=q_sq[:, 0:1], in1=neg_a, op0=add, op1=mult
                    ),
                ],
            ]
            projection = [
                [lambda: vec.tensor_scalar_max(out=den_clamped[:], in0=den[:], scalar1=EPS)],
                [
                    lambda: vec.reciprocal(out=inv_den[:], in_=den_clamped[:]),
                    lambda: vec.scalar_tensor_tensor(
                        out=excess[:], in0=mm_den[:], scalar=-1.0 / 3.0, in1=den_clamped[:],
                        op0=mult, op1=add,
                    ),
                ],
                [
                    lambda: vec.scalar_tensor_tensor(
                        out=neg_shrink[:], in0=excess[:], scalar=-1.5 * MAXN, in1=inv_den[:],
                        op0=mult, op1=mult,
                    )
                ],
                [
                    lambda: vec.scalar_tensor_tensor(
                        out=neg_common[:, 0, :], in0=neg_shrink[:], scalar=-1.0, in1=inv_den[:],
                        op0=ALU.max, op1=mult,
                    )
                ],
                [
                    lambda: vec.tensor_mul(
                        out=coefs[:, b, :, :], in0=terms[:, 0:2, :],
                        in1=neg_common[:].to_broadcast([P, 2, BATCH]),
                    )
                ],
            ]
            return norms_and_rho + while_gpsimd_works + moebius + projection

        rounds = {}

        def issue_rounds(s, early):
            for b in sorted(rounds):
                k = 2 * (s + 1 - DOT_BEHIND - (b + 1) * BATCH) - early
                if 0 <= k < len(rounds[b]):
                    for issue in rounds[b][k]:
                        issue()

        q_rows = {}
        result = {}

        def scale_q(t, on_scalar):
            q_rows[t] = bias_rows.tile([P, D], F32, name="q_row")
            if on_scalar:
                nc.scalar.activation(
                    out=q_rows[t][:], in_=q_all[:], func=ACT.Copy,
                    scale=coefs[:, t // BATCH, 1, t % BATCH : t % BATCH + 1],
                )
            else:
                nc.gpsimd.tensor_scalar(
                    out=q_rows[t][:], in0=q_all[:],
                    scalar1=coefs[:, t // BATCH, 1, t % BATCH : t % BATCH + 1], scalar2=0.0,
                    op0=ALU.mult, op1=ALU.add,
                )

        def write_tile(t):
            g, j = divmod(t, GROUP)
            if j == 0:
                result[g] = results.tile([P, GROUP, D], F32, name="result")
            acc_b = psum.tile([P, D], F32, name="bank")
            product(acc_b[:], t)
            nc.vector.scalar_tensor_tensor(
                out=result[g][:, j, :], in0=acc_b[:],
                scalar=coefs[:, t // BATCH, 0, t % BATCH : t % BATCH + 1], in1=q_rows[t][:],
                op0=ALU.mult, op1=ALU.subtract,
            )
            if j == GROUP - 1:
                tiles = slice(g * GROUP, (g + 1) * GROUP)
                nc.sync.dma_start(out=out_rows[:, tiles, :], in_=result[g][:])

        b_sq, b_sq_clamped, b_norm = small("b_sq", 1), small("b_sq_clamped", 1), small("b_norm", 1)
        b_exponent, b_power = small("b_exponent", 1), small("b_power", 1)
        b_above, b_below, b_inv_below = small("b_above", 1), small("b_below", 1), small("b_inv_below", 1)
        q_scale = small("q_scale", 1)
        def sum_squares_on_vector(t):
            squares = unread.tile([P, D], F32, name="by_vector")
            nc.vector.scalar_tensor_tensor(
                out=squares[:], in0=x_sb[:, t, :], scalar=1.0, in1=x_sb[:, t, :],
                op0=ALU.mult, op1=ALU.mult, accum_out=sums[:, 0, t : t + 1],
            )

        transpose_group(0)
        regroup_half(0, 0, True)
        regroup_half(0, 1, True)
        for t in range(X_AHEAD - 2):
            sum_squares(x_sb[:, t, :], sums[:, 0, t : t + 1])
        b_all = psum.tile([P, D], F32, name="bank")
        nc.tensor.matmul(out=b_all[:], lhsT=ones[:], rhs=b_row[:], start=True, stop=True)
        sum_squares(b_all[:], b_sq[:])
        sum_squares_on_vector(X_AHEAD - 2)
        quantise_group(0)
        nc.vector.tensor_scalar_max(out=b_sq_clamped[:], in0=b_sq[:], scalar1=EPS)
        nc.scalar.activation(out=b_norm[:], in_=b_sq_clamped[:], func=ACT.Sqrt)
        transpose_group(1)
        regroup_half(1, 0, True)
        nc.vector.tensor_scalar_mul(out=b_exponent[:], in0=b_norm[:], scalar1=TWO_LOG2E)
        nc.gpsimd.tensor_tensor(out=b_power[:], in0=two[:], in1=b_exponent[:], op=ALU.pow)
        regroup_half(1, 1, True)
        sum_squares_on_vector(X_AHEAD - 1)
        nc.vector.tensor_scalar_add(out=b_above[:], in0=b_power[:], scalar1=-1.0)
        nc.vector.scalar_tensor_tensor(
            out=b_below[:], in0=b_power[:], scalar=1.0, in1=b_norm[:], op0=ALU.add, op1=ALU.mult
        )
        quantise_group(1)
        nc.vector.reciprocal(out=b_inv_below[:], in_=b_below[:])
        nc.vector.tensor_mul(out=q_scale[:], in0=b_above[:], in1=b_inv_below[:])
        nc.vector.tensor_scalar_mul(out=q_all[:], in0=b_all[:], scalar1=q_scale[:, 0:1])

        def by_gram(t):
            return GRAM_FIRST <= t < GRAM_FIRST + GRAM_TILES

        grams = {}

        def gram(t):
            g, j = divmod(t, GROUP)
            grams[t] = psum.tile([P, P], F32, name="bank")
            for c in range(PACK):
                x_t = regrouped[g][:, j, :, c]
                nc.tensor.matmul(out=grams[t][:], lhsT=x_t, rhs=x_t, start=(c == 0), stop=(c == PACK - 1))

        def sum_diagonal(t):
            masked = unread.tile([P, D], F32, name="by_vector")
            nc.vector.scalar_tensor_tensor(
                out=masked[:, 0:P], in0=grams[t][:], scalar=1.0, in1=ident[:], op0=ALU.mult, op1=ALU.mult,
                accum_out=sums[:, 0, t : t + 1],
            )

        def written(s):
            if s < TILES - HOLD:
                return s - LAG if s >= LAG else None
            if s < TILES:
                return None
            return s - LAG - HOLD if s - LAG - HOLD < TILES else None

        def slot_of(t):
            return t + LAG if t + LAG < TILES - HOLD else t + LAG + HOLD

        def known(b):
            return (b + 1) * BATCH - 1 + DOT_BEHIND + ROUNDS // 2 + (HOLD if b == BATCHES - 1 else 0)

        accs = {}
        for s in range(TILES + LAG + HOLD):
            if s + X_AHEAD < TILES and not by_gram(s + X_AHEAD):
                if s < LAG and s % 8 == 7:
                    sum_squares_on_vector(s + X_AHEAD)
                else:
                    sum_squares(x_sb[:, s + X_AHEAD, :], sums[:, 0, s + X_AHEAD : s + X_AHEAD + 1])
            if s < TILES:
                accs[s] = psum.tile([P, D], F32, name="bank")
                product(accs[s][:], s)
                sum_squares(accs[s][:], sums[:, 1, s : s + 1])
            if by_gram(s + GRAM_AHEAD):
                gram(s + GRAM_AHEAD)
            if DOT_BEHIND <= s < TILES + DOT_BEHIND:
                sum_mx_times_q(accs[s - DOT_BEHIND][:], s - DOT_BEHIND)
            if by_gram(s + GRAM_AHEAD - 1):
                sum_diagonal(s + GRAM_AHEAD - 1)
            issue_rounds(s, 1)
            if written(s) is not None:
                write_tile(written(s))
            if s < TILES:
                g, j = divmod(s, GROUP)
                if j == 0 and FEED_AHEAD <= g - 1 + FEED_AHEAD < GROUPS:
                    quantise_group(g - 1 + FEED_AHEAD)
                if g + FEED_AHEAD < GROUPS:
                    if j == 0:
                        transpose_group(g + FEED_AHEAD)
                    elif j < GROUP - 1:
                        regroup_half(g + FEED_AHEAD, j - 1, s < LAG and not by_gram(s + X_AHEAD))
            started, since = divmod(s + 1 - DOT_BEHIND, BATCH)
            if since == 0 and 1 <= started <= BATCHES:
                last = started == BATCHES
                rounds[started - 1] = coefficient_rounds(started - 1, POW_ROUNDS + (2 * HOLD if last else 0))
            issue_rounds(s, 0)
            if s == GROUP:
                sum_squares(q_all[:], q_sq[:])
                nc.vector.tensor_scalar_add(out=q_sq_m1[:], in0=q_sq[:], scalar1=-1.0)
            for t in range(TILES):
                if t not in q_rows and known(t // BATCH) <= s and slot_of(t) <= s + Q_ROWS_MOST:
                    scale_q(t, s >= TILES)
